import numpy as np
import ml_dtypes


def mxq(x, axis, fmt="e4m3"):
    dtype, down = {"e4m3": (ml_dtypes.float8_e4m3fn, 7), "e5m2": (ml_dtypes.float8_e5m2, 14)}[fmt]
    v = np.moveaxis(np.asarray(x, np.float32).astype(ml_dtypes.bfloat16).astype(np.float64), axis, -1)
    blocks = v.reshape(v.shape[:-1] + (-1, 32))
    amax = np.abs(blocks).max(-1, keepdims=True)
    byte = np.maximum(np.where(amax > 0, np.frexp(amax)[1] - 1 + 127, 0) - down, 1)
    scale = np.exp2(byte - 127.0)
    codes = (blocks / scale).astype(np.float32).astype(dtype).astype(np.float64)
    return np.moveaxis((codes * scale).reshape(v.shape), -1, axis)


WIDE = False


def mx_kscale(k):
    if not WIDE:
        return np.ones(k)
    levels = np.array([10, -10, 5, -5, 0])
    a = np.random.permutation(np.resize(levels, k // 512 * 4)).reshape(k // 512, 4)
    idx = np.arange(k)
    return np.exp2(a[idx // 512, idx % 128 // 32])


BF16 = ml_dtypes.bfloat16


def bf(x):
    return np.asarray(x, np.float32).astype(BF16)


def f64(x):
    return np.asarray(x).astype(np.float64)


E2M1 = np.array([0.0, 0.5, 1.0, 1.5, 2.0, 3.0, 4.0, 6.0, -0.0, -0.5, -1.0, -1.5, -2.0, -3.0, -4.0, -6.0])


def pack_weight(w, fmt):
    k, n = w.shape
    w = f64(bf(w)).reshape(k // 32, 32, n)
    amax = np.abs(w).max(1)
    if fmt == "e4m3":
        byte = np.frexp(amax)[1] - 1 + 127 - 7
    else:
        mant, ex = np.frexp(amax / 6.0)
        byte = np.where(mant > 0.5, ex, ex - 1) + 127
    byte = np.clip(np.where(amax > 0, byte, 1), 1, 254)
    scaled = (w * np.exp2(127.0 - byte)[:, None, :]).reshape(k, n).astype(np.float32)
    by_word = np.ascontiguousarray(scaled.reshape(k // 512, 128, 4, n).transpose(0, 1, 3, 2))
    if fmt == "e4m3":
        words = by_word.astype(ml_dtypes.float8_e4m3fn).view(np.uint8)
    else:
        c = by_word.astype(ml_dtypes.float4_e2m1fn).view(np.uint8) & 0xF
        words = c[..., 0::2] | (c[..., 1::2] << 4)
    return np.ascontiguousarray(words), np.ascontiguousarray(byte.astype(np.uint8).reshape(k // 512, 16, n))


def unpack_weight(words, scales, fmt):
    g, p, n, _ = words.shape
    if fmt == "e4m3":
        vals = np.ascontiguousarray(words).view(ml_dtypes.float8_e4m3fn).astype(np.float64)
    else:
        nib = np.empty((g, p, n, 4), np.uint8)
        nib[..., 0::2] = words & 0xF
        nib[..., 1::2] = words >> 4
        vals = E2M1[nib]
    vals = vals * np.repeat(np.exp2(scales.astype(np.float64) - 127.0), 8, axis=1)[..., None]
    return vals.transpose(0, 1, 3, 2).reshape(g * 512, n)

def pack4(w):
    words, scales = pack_weight(w, "e2m1")
    return words.reshape(words.shape[0], 128, -1), scales


def unpack4(words, scales):
    return unpack_weight(words.reshape(words.shape[0], 128, -1, 2), scales, "e2m1")


B, N, D, DO, H, HID = 64, 128, 512, 256, 8, 2048


def setup_inputs():
    s, t = mx_kscale(D), mx_kscale(D)
    adj = np.random.uniform(size=(N, N))
    adj = adj / adj.sum(-1, keepdims=True)
    h_norm = bf(np.random.standard_normal((B, N, D)) * s)
    o_attn = bf(np.random.standard_normal((B, N, D)) * 0.25 * t)
    a_gcn = bf(adj + np.random.standard_normal((N, N)) * 0.5 / np.sqrt(N))
    w_proj_words, w_proj_scales = pack4(np.random.standard_normal((D, DO)) * 2.0 / np.sqrt(D) / t[:, None])
    b_proj = bf(np.random.standard_normal(DO) * 0.1)
    gcn_w_words, gcn_w_scales = pack4(np.random.standard_normal((D, DO)) / np.sqrt(D) / s[:, None])
    gcn_m = bf(1.0 + 0.1 * np.random.standard_normal(DO))
    return {
        "h_norm": h_norm,
        "o_attn": o_attn,
        "a_gcn": a_gcn,
        "w_proj_words": w_proj_words,
        "w_proj_scales": w_proj_scales,
        "b_proj": b_proj,
        "gcn_w_words": gcn_w_words,
        "gcn_w_scales": gcn_w_scales,
        "gcn_m": gcn_m,
    }


def reference(h_norm, o_attn, a_gcn, w_proj_words, w_proj_scales, b_proj, gcn_w_words, gcn_w_scales, gcn_m):
    o = (mxq(f64(o_attn), 2, "e4m3") @ unpack4(w_proj_words, w_proj_scales)) + f64(b_proj)
    agg = f64(a_gcn) @ f64(h_norm)
    g = (mxq(agg, 2, "e4m3") @ unpack4(gcn_w_words, gcn_w_scales)) * f64(gcn_m)
    return o + g

@@ -1,0 +1,169 @@
+from contextlib import ExitStack
+
+import concourse.mybir as mybir
+from concourse.masks import make_identity
+
+BF16 = mybir.dt.bfloat16
+F32 = mybir.dt.float32
+I32 = mybir.dt.int32
+U8 = mybir.dt.uint8
+U32 = mybir.dt.uint32
+FP8X4 = mybir.dt.float8_e4m3fn_x4
+FP4X4 = mybir.dt.float4_e2m1fn_x4
+MULT = mybir.AluOpType.mult
+ADD = mybir.AluOpType.add
+
+P = 128
+PACK = 4
+SAMPLES = 64
+D = 512
+DO = 256
+PAIR = 2
+N_PAIRS = SAMPLES // PAIR
+AHEAD = 6
+PROJ, GCN = 0, 1
+
+FLOPS = 2 * SAMPLES * P * D * DO * 2 + 2 * SAMPLES * P * P * D
+
+
+def tile_gatblock_pa_t_kernel(
+    tc,
+    h_norm,
+    o_attn,
+    a_gcn,
+    w_proj_words,
+    w_proj_scales,
+    b_proj,
+    gcn_w_words,
+    gcn_w_scales,
+    gcn_m,
+    out,
+):
+    nc = tc.nc
+    with ExitStack() as pools:
+        const = pools.enter_context(tc.tile_pool(name="const", bufs=1))
+        loads = pools.enter_context(tc.tile_pool(name="loads", bufs=AHEAD + 2))
+        work = pools.enter_context(tc.tile_pool(name="work", bufs=3))
+        psum_agg = pools.enter_context(tc.psum_pool(name="psum_agg", bufs=4))
+        psum_words = pools.enter_context(tc.psum_pool(name="psum_words", bufs=2))
+        psum_out = pools.enter_context(tc.psum_pool(name="psum_out", bufs=1))
+
+        loaded = {}
+
+        def load(k):
+            samples = slice(k * PAIR, (k + 1) * PAIR)
+            h_sb = loads.tile([P, PAIR, D], BF16)
+            nc.sync.dma_start(out=h_sb[:], in_=h_norm[samples].rearrange("b j d -> j b d"))
+            o_sb = loads.tile([P, PAIR, D], BF16)
+            nc.sync.dma_start(out=o_sb[:], in_=o_attn[samples].rearrange("b i d -> i b d"))
+            loaded[k] = (h_sb, o_sb)
+
+        a_sb = const.tile([P, P], BF16)
+        nc.sync.dma_start(out=a_sb[:], in_=a_gcn)
+        load(0)
+
+        w_words = const.tile([P, 2, 2 * DO], U8, align_bytes=64)
+        w_planes = const.tile([P, 2, DO], U8, align_bytes=64)
+        nc.vector.memset(w_planes[:].rearrange("p w n -> p (w n)").bitcast(I32), 0)
+        for branch, words, scales in ((PROJ, w_proj_words, w_proj_scales), (GCN, gcn_w_words, gcn_w_scales)):
+            nc.sync.dma_start(out=w_words[:, branch, :].bitcast(I32), in_=words[0].bitcast(I32))
+            for quadrant in range(4):
+                nc.sync.dma_start(
+                    out=w_planes[32 * quadrant : 32 * quadrant + 4, branch, :].bitcast(I32),
+                    in_=scales[0, 4 * quadrant : 4 * quadrant + 4, :].bitcast(I32),
+                )
+
+        bias_bf = const.tile([P, DO], BF16)
+        nc.scalar.dma_start(out=bias_bf[:], in_=b_proj.partition_broadcast(P))
+        gain_bf = const.tile([P, DO], BF16)
+        nc.scalar.dma_start(out=gain_bf[:], in_=gcn_m.partition_broadcast(P))
+        bias = const.tile([P, DO], F32)
+        nc.vector.tensor_copy(out=bias[:], in_=bias_bf[:])
+        gain = const.tile([P, DO], F32)
+        nc.vector.tensor_copy(out=gain[:], in_=gain_bf[:])
+
+        ident_bf = const.tile([P, P], BF16)
+        make_identity(nc, ident_bf[:])
+        ident_f32 = const.tile([P, P], F32)
+        make_identity(nc, ident_f32[:])
+
+        aT_ps = psum_words.tile([P, P], BF16, tag="oT_ps")
+        nc.tensor.transpose(aT_ps[:], a_sb[:], ident_bf[:])
+        aT = const.tile([P, P], BF16)
+        nc.vector.tensor_copy(out=aT[:], in_=aT_ps[:])
+
+        quantised = {}
+
+        def quantise(k):
+            h_sb, o_sb = loaded.pop(k)
+            grouped = work.tile([P, 2, PAIR, D], BF16, align_bytes=64)
+
+            oT_ps = psum_words.tile([P, PAIR, 2, P], F32)
+            for s in range(PAIR):
+                o_words = o_sb[:, s, :].bitcast(F32)
+                for u in range(2):
+                    nc.tensor.transpose(oT_ps[:, s, u, :], o_words[:, u : D // 2 : 2], ident_f32[:])
+            nc.scalar.copy(
+                out=grouped[:, PROJ].bitcast(F32).rearrange("p s (i u) -> p s i u", u=2),
+                in_=oT_ps[:].rearrange("p s u i -> p s i u"),
+            )
+
+            for s in range(PAIR):
+                aggT_ps = psum_agg.tile([P, PACK, P], F32)
+                for t in range(PACK):
+                    nc.tensor.matmul(
+                        aggT_ps[:, t, :], lhsT=h_sb[:, s, t:D:PACK], rhs=aT[:], start=True, stop=True
+                    )
+                nc.scalar.copy(
+                    out=grouped[:, GCN, s, :].rearrange("p (i t) -> p i t", t=PACK),
+                    in_=aggT_ps[:].rearrange("p t i -> p i t"),
+                )
+
+            codes = work.tile([P, 2 * PAIR * P], U32, align_bytes=64)
+            scales = work.tile([P, 2 * PAIR * P], U8, align_bytes=64)
+            nc.vector.quantize_mx(
+                out=codes[:].bitcast(FP8X4),
+                scales=scales[:],
+                in_=grouped[:].rearrange("p a s k -> p (a s k)"),
+            )
+            quantised[k] = (codes, scales)
+
+        def finish(k):
+            codes, scales = quantised.pop(k)
+            o_ps = psum_out.tile([P, PAIR, DO], F32)
+            g_ps = psum_out.tile([P, PAIR, DO], F32)
+            for branch, product in ((GCN, g_ps), (PROJ, o_ps)):
+                for s in range(PAIR):
+                    nodes = slice((branch * PAIR + s) * P, (branch * PAIR + s + 1) * P)
+                    nc.tensor.matmul_mx(
+                        out=product[:, s, :],
+                        lhsT=codes[:, nodes].bitcast(FP8X4),
+                        lhsT_scale=scales[:, nodes],
+                        rhs=w_words[:, branch, :].bitcast(FP4X4),
+                        rhs_scale=w_planes[:, branch, :],
+                        start=True,
+                        stop=True,
+                    )
+            g_scaled = work.tile([P, PAIR, DO], F32)
+            nc.vector.tensor_tensor(
+                out=g_scaled[:], in0=g_ps[:], in1=gain[:].unsqueeze(1).to_broadcast([P, PAIR, DO]), op=MULT
+            )
+            o_biased = work.tile([P, PAIR, DO], F32)
+            nc.vector.tensor_tensor(
+                out=o_biased[:], in0=o_ps[:], in1=bias[:].unsqueeze(1).to_broadcast([P, PAIR, DO]), op=ADD
+            )
+            result = work.tile([P, PAIR, DO], F32)
+            nc.gpsimd.tensor_tensor(out=result[:], in0=g_scaled[:], in1=o_biased[:], op=ADD)
+            nc.sync.dma_start(
+                out=out[k * PAIR : (k + 1) * PAIR].rearrange("b i n -> i b n"), in_=result[:]
+            )
+
+        for k in range(1, AHEAD):
+            load(k)
+        for k in range(N_PAIRS + 1):
+            if k + AHEAD < N_PAIRS:
+                load(k + AHEAD)
+            if k < N_PAIRS:
+                quantise(k)
+            if k >= 1:
+                finish(k - 1)

@@ -40,15 +40,19 @@ def tile_gatblock_pa_t_kernel(
     out,
 ):
     nc = tc.nc
-    with ExitStack() as pools:
-        const = pools.enter_context(tc.tile_pool(name="const", bufs=1))
-        loads = pools.enter_context(tc.tile_pool(name="loads", bufs=AHEAD + 2))
-        work = pools.enter_context(tc.tile_pool(name="work", bufs=3))
-        psum_agg = pools.enter_context(tc.psum_pool(name="psum_agg", bufs=4))
-        psum_words = pools.enter_context(tc.psum_pool(name="psum_words", bufs=2))
-        psum_out = pools.enter_context(tc.psum_pool(name="psum_out", bufs=1))
+    with ExitStack() as stack:
+        const = stack.enter_context(tc.tile_pool(name="const", bufs=1))
+        loads = stack.enter_context(tc.tile_pool(name="loads", bufs=AHEAD + 2))
+        work = stack.enter_context(tc.tile_pool(name="work", bufs=4))
+        psum_agg = stack.enter_context(tc.psum_pool(name="psum_agg", bufs=4))
+        psum_words = stack.enter_context(tc.psum_pool(name="psum_words", bufs=2))
+        psum_out = stack.enter_context(tc.psum_pool(name="psum_out", bufs=1))
+        stack.enter_context(tc.manual_schedule())
 
         loaded = {}
+        grouped_tiles = {}
+        quantised = {}
+        products = {}
 
         def load(k):
             samples = slice(k * PAIR, (k + 1) * PAIR)
@@ -61,6 +65,7 @@ def tile_gatblock_pa_t_kernel(
         a_sb = const.tile([P, P], BF16)
         nc.sync.dma_start(out=a_sb[:], in_=a_gcn)
         load(0)
+        load(1)
 
         w_words = const.tile([P, 2, 2 * DO], U8, align_bytes=64)
         w_planes = const.tile([P, 2, DO], U8, align_bytes=64)
@@ -72,15 +77,8 @@ def tile_gatblock_pa_t_kernel(
                     out=w_planes[32 * quadrant : 32 * quadrant + 4, branch, :].bitcast(I32),
                     in_=scales[0, 4 * quadrant : 4 * quadrant + 4, :].bitcast(I32),
                 )
-
-        bias_bf = const.tile([P, DO], BF16)
-        nc.scalar.dma_start(out=bias_bf[:], in_=b_proj.partition_broadcast(P))
-        gain_bf = const.tile([P, DO], BF16)
-        nc.scalar.dma_start(out=gain_bf[:], in_=gcn_m.partition_broadcast(P))
-        bias = const.tile([P, DO], F32)
-        nc.vector.tensor_copy(out=bias[:], in_=bias_bf[:])
-        gain = const.tile([P, DO], F32)
-        nc.vector.tensor_copy(out=gain[:], in_=gain_bf[:])
+        for k in range(2, AHEAD):
+            load(k)
 
         ident_bf = const.tile([P, P], BF16)
         make_identity(nc, ident_bf[:])
@@ -92,9 +90,16 @@ def tile_gatblock_pa_t_kernel(
         aT = const.tile([P, P], BF16)
         nc.vector.tensor_copy(out=aT[:], in_=aT_ps[:])
 
-        quantised = {}
+        bias_bf = const.tile([P, DO], BF16)
+        nc.scalar.dma_start(out=bias_bf[:], in_=b_proj.partition_broadcast(P))
+        gain_bf = const.tile([P, DO], BF16)
+        nc.scalar.dma_start(out=gain_bf[:], in_=gcn_m.partition_broadcast(P))
+        bias = const.tile([P, DO], F32)
+        nc.vector.tensor_copy(out=bias[:], in_=bias_bf[:])
+        gain = const.tile([P, DO], F32)
+        nc.vector.tensor_copy(out=gain[:], in_=gain_bf[:])
 
-        def quantise(k):
+        def transpose_and_mix(k):
             h_sb, o_sb = loaded.pop(k)
             grouped = work.tile([P, 2, PAIR, D], BF16, align_bytes=64)
 
@@ -118,7 +123,10 @@ def tile_gatblock_pa_t_kernel(
                     out=grouped[:, GCN, s, :].rearrange("p (i t) -> p i t", t=PACK),
                     in_=aggT_ps[:].rearrange("p t i -> p i t"),
                 )
+            grouped_tiles[k] = grouped
 
+        def quantise(k):
+            grouped = grouped_tiles.pop(k)
             codes = work.tile([P, 2 * PAIR * P], U32, align_bytes=64)
             scales = work.tile([P, 2 * PAIR * P], U8, align_bytes=64)
             nc.vector.quantize_mx(
@@ -128,10 +136,10 @@ def tile_gatblock_pa_t_kernel(
             )
             quantised[k] = (codes, scales)
 
-        def finish(k):
+        def multiply(k):
             codes, scales = quantised.pop(k)
-            o_ps = psum_out.tile([P, PAIR, DO], F32)
             g_ps = psum_out.tile([P, PAIR, DO], F32)
+            o_ps = psum_out.tile([P, PAIR, DO], F32)
             for branch, product in ((GCN, g_ps), (PROJ, o_ps)):
                 for s in range(PAIR):
                     nodes = slice((branch * PAIR + s) * P, (branch * PAIR + s + 1) * P)
@@ -144,6 +152,10 @@ def tile_gatblock_pa_t_kernel(
                         start=True,
                         stop=True,
                     )
+            products[k] = (g_ps, o_ps)
+
+        def epilogue(k):
+            g_ps, o_ps = products.pop(k)
             g_scaled = work.tile([P, PAIR, DO], F32)
             nc.vector.tensor_tensor(
                 out=g_scaled[:], in0=g_ps[:], in1=gain[:].unsqueeze(1).to_broadcast([P, PAIR, DO]), op=MULT
@@ -158,12 +170,14 @@ def tile_gatblock_pa_t_kernel(
                 out=out[k * PAIR : (k + 1) * PAIR].rearrange("b i n -> i b n"), in_=result[:]
             )
 
-        for k in range(1, AHEAD):
-            load(k)
-        for k in range(N_PAIRS + 1):
-            if k + AHEAD < N_PAIRS:
-                load(k + AHEAD)
-            if k < N_PAIRS:
-                quantise(k)
-            if k >= 1:
-                finish(k - 1)
+        for i in range(N_PAIRS + 2):
+            if i + AHEAD < N_PAIRS:
+                load(i + AHEAD)
+            if i >= 2:
+                multiply(i - 2)
+            if i < N_PAIRS:
+                transpose_and_mix(i)
+            if i >= 2:
+                epilogue(i - 2)
+            if 1 <= i <= N_PAIRS:
+                quantise(i - 1)

@@ -170,14 +170,14 @@ def tile_gatblock_pa_t_kernel(
                 out=out[k * PAIR : (k + 1) * PAIR].rearrange("b i n -> i b n"), in_=result[:]
             )
 
-        for i in range(N_PAIRS + 2):
+        for i in range(N_PAIRS + 3):
             if i + AHEAD < N_PAIRS:
                 load(i + AHEAD)
-            if i >= 2:
-                multiply(i - 2)
+            if i >= 3:
+                epilogue(i - 3)
             if i < N_PAIRS:
                 transpose_and_mix(i)
-            if i >= 2:
-                epilogue(i - 2)
             if 1 <= i <= N_PAIRS:
                 quantise(i - 1)
+            if 2 <= i <= N_PAIRS + 1:
+                multiply(i - 2)

@@ -50,6 +50,7 @@ def tile_gatblock_pa_t_kernel(
         stack.enter_context(tc.manual_schedule())
 
         loaded = {}
+        sorted_tiles = {}
         grouped_tiles = {}
         quantised = {}
         products = {}
@@ -99,8 +100,18 @@ def tile_gatblock_pa_t_kernel(
         gain = const.tile([P, DO], F32)
         nc.vector.tensor_copy(out=gain[:], in_=gain_bf[:])
 
+        def sort_h(k):
+            h_sb = loaded[k][0]
+            h_sorted = work.tile([P, PAIR, 2, D // 2], BF16)
+            nc.vector.tensor_copy(
+                out=h_sorted[:].bitcast(F32),
+                in_=h_sb[:].bitcast(F32).rearrange("j s (p u) -> j s u p", u=2),
+            )
+            sorted_tiles[k] = h_sorted
+
         def transpose_and_mix(k):
-            h_sb, o_sb = loaded.pop(k)
+            o_sb = loaded.pop(k)[1]
+            h_sorted = sorted_tiles.pop(k)
             grouped = work.tile([P, 2, PAIR, D], BF16, align_bytes=64)
 
             oT_ps = psum_words.tile([P, PAIR, 2, P], F32)
@@ -116,8 +127,9 @@ def tile_gatblock_pa_t_kernel(
             for s in range(PAIR):
                 aggT_ps = psum_agg.tile([P, PACK, P], F32)
                 for t in range(PACK):
+                    u, e = divmod(t, 2)
                     nc.tensor.matmul(
-                        aggT_ps[:, t, :], lhsT=h_sb[:, s, t:D:PACK], rhs=aT[:], start=True, stop=True
+                        aggT_ps[:, t, :], lhsT=h_sorted[:, s, u, e : D // 2 : 2], rhs=aT[:], start=True, stop=True
                     )
                 nc.scalar.copy(
                     out=grouped[:, GCN, s, :].rearrange("p (i t) -> p i t", t=PACK),
@@ -170,6 +182,7 @@ def tile_gatblock_pa_t_kernel(
                 out=out[k * PAIR : (k + 1) * PAIR].rearrange("b i n -> i b n"), in_=result[:]
             )
 
+        sort_h(0)
         for i in range(N_PAIRS + 3):
             if i + AHEAD < N_PAIRS:
                 load(i + AHEAD)
@@ -179,5 +192,7 @@ def tile_gatblock_pa_t_kernel(
                 transpose_and_mix(i)
             if 1 <= i <= N_PAIRS:
                 quantise(i - 1)
+            if i + 1 < N_PAIRS:
+                sort_h(i + 1)
             if 2 <= i <= N_PAIRS + 1:
                 multiply(i - 2)

@@ -50,17 +50,18 @@ def tile_gatblock_pa_t_kernel(
         stack.enter_context(tc.manual_schedule())
 
         loaded = {}
-        sorted_tiles = {}
         grouped_tiles = {}
         quantised = {}
         products = {}
 
+        o_rows = o_attn.flatten_outer_dims().rearrange("(k p r) d -> k p r d", p=P, r=PAIR)
+        out_rows = out.flatten_outer_dims().rearrange("(k p r) n -> k p r n", p=P, r=PAIR)
+
         def load(k):
-            samples = slice(k * PAIR, (k + 1) * PAIR)
             h_sb = loads.tile([P, PAIR, D], BF16)
-            nc.sync.dma_start(out=h_sb[:], in_=h_norm[samples].rearrange("b j d -> j b d"))
+            nc.sync.dma_start(out=h_sb[:], in_=h_norm[k * PAIR : (k + 1) * PAIR].rearrange("b j d -> j b d"))
             o_sb = loads.tile([P, PAIR, D], BF16)
-            nc.sync.dma_start(out=o_sb[:], in_=o_attn[samples].rearrange("b i d -> i b d"))
+            nc.sync.dma_start(out=o_sb[:], in_=o_rows[k])
             loaded[k] = (h_sb, o_sb)
 
         a_sb = const.tile([P, P], BF16)
@@ -100,40 +101,29 @@ def tile_gatblock_pa_t_kernel(
         gain = const.tile([P, DO], F32)
         nc.vector.tensor_copy(out=gain[:], in_=gain_bf[:])
 
-        def sort_h(k):
-            h_sb = loaded[k][0]
-            h_sorted = work.tile([P, PAIR, 2, D // 2], BF16)
-            nc.vector.tensor_copy(
-                out=h_sorted[:].bitcast(F32),
-                in_=h_sb[:].bitcast(F32).rearrange("j s (p u) -> j s u p", u=2),
-            )
-            sorted_tiles[k] = h_sorted
-
         def transpose_and_mix(k):
-            o_sb = loaded.pop(k)[1]
-            h_sorted = sorted_tiles.pop(k)
+            h_sb, o_sb = loaded.pop(k)
             grouped = work.tile([P, 2, PAIR, D], BF16, align_bytes=64)
 
             oT_ps = psum_words.tile([P, PAIR, 2, P], F32)
-            for s in range(PAIR):
-                o_words = o_sb[:, s, :].bitcast(F32)
+            for r in range(PAIR):
+                o_words = o_sb[:, r, :].bitcast(F32)
                 for u in range(2):
-                    nc.tensor.transpose(oT_ps[:, s, u, :], o_words[:, u : D // 2 : 2], ident_f32[:])
+                    nc.tensor.transpose(oT_ps[:, r, u, :], o_words[:, u : D // 2 : 2], ident_f32[:])
             nc.scalar.copy(
-                out=grouped[:, PROJ].bitcast(F32).rearrange("p s (i u) -> p s i u", u=2),
-                in_=oT_ps[:].rearrange("p s u i -> p s i u"),
+                out=grouped[:, PROJ].bitcast(F32).rearrange("p r (c u) -> p r c u", u=2),
+                in_=oT_ps[:].rearrange("p r u c -> p r c u"),
             )
 
             for s in range(PAIR):
                 aggT_ps = psum_agg.tile([P, PACK, P], F32)
                 for t in range(PACK):
-                    u, e = divmod(t, 2)
                     nc.tensor.matmul(
-                        aggT_ps[:, t, :], lhsT=h_sorted[:, s, u, e : D // 2 : 2], rhs=aT[:], start=True, stop=True
+                        aggT_ps[:, t, :], lhsT=h_sb[:, s, t:D:PACK], rhs=aT[:], start=True, stop=True
                     )
                 nc.scalar.copy(
-                    out=grouped[:, GCN, s, :].rearrange("p (i t) -> p i t", t=PACK),
-                    in_=aggT_ps[:].rearrange("p t i -> p i t"),
+                    out=grouped[:, GCN, :, s * D // PAIR : (s + 1) * D // PAIR].rearrange("p r (c t) -> p r c t", t=PACK),
+                    in_=aggT_ps[:].rearrange("p t (c r) -> p r c t", r=PAIR),
                 )
             grouped_tiles[k] = grouped
 
@@ -144,7 +134,7 @@ def tile_gatblock_pa_t_kernel(
             nc.vector.quantize_mx(
                 out=codes[:].bitcast(FP8X4),
                 scales=scales[:],
-                in_=grouped[:].rearrange("p a s k -> p (a s k)"),
+                in_=grouped[:].rearrange("p a r k -> p (a r k)"),
             )
             quantised[k] = (codes, scales)
 
@@ -153,12 +143,12 @@ def tile_gatblock_pa_t_kernel(
             g_ps = psum_out.tile([P, PAIR, DO], F32)
             o_ps = psum_out.tile([P, PAIR, DO], F32)
             for branch, product in ((GCN, g_ps), (PROJ, o_ps)):
-                for s in range(PAIR):
-                    nodes = slice((branch * PAIR + s) * P, (branch * PAIR + s + 1) * P)
+                for r in range(PAIR):
+                    half = slice((branch * PAIR + r) * P, (branch * PAIR + r + 1) * P)
                     nc.tensor.matmul_mx(
-                        out=product[:, s, :],
-                        lhsT=codes[:, nodes].bitcast(FP8X4),
-                        lhsT_scale=scales[:, nodes],
+                        out=product[:, r, :],
+                        lhsT=codes[:, half].bitcast(FP8X4),
+                        lhsT_scale=scales[:, half],
                         rhs=w_words[:, branch, :].bitcast(FP4X4),
                         rhs_scale=w_planes[:, branch, :],
                         start=True,
@@ -178,11 +168,8 @@ def tile_gatblock_pa_t_kernel(
             )
             result = work.tile([P, PAIR, DO], F32)
             nc.gpsimd.tensor_tensor(out=result[:], in0=g_scaled[:], in1=o_biased[:], op=ADD)
-            nc.sync.dma_start(
-                out=out[k * PAIR : (k + 1) * PAIR].rearrange("b i n -> i b n"), in_=result[:]
-            )
+            nc.sync.dma_start(out=out_rows[k], in_=result[:])
 
-        sort_h(0)
         for i in range(N_PAIRS + 3):
             if i + AHEAD < N_PAIRS:
                 load(i + AHEAD)
@@ -192,7 +179,5 @@ def tile_gatblock_pa_t_kernel(
                 transpose_and_mix(i)
             if 1 <= i <= N_PAIRS:
                 quantise(i - 1)
-            if i + 1 < N_PAIRS:
-                sort_h(i + 1)
             if 2 <= i <= N_PAIRS + 1:
                 multiply(i - 2)

@@ -101,8 +101,8 @@ def tile_gatblock_pa_t_kernel(
         gain = const.tile([P, DO], F32)
         nc.vector.tensor_copy(out=gain[:], in_=gain_bf[:])
 
-        def transpose_and_mix(k):
-            h_sb, o_sb = loaded.pop(k)
+        def transposes(k):
+            h_sb, o_sb = loaded[k]
             grouped = work.tile([P, 2, PAIR, D], BF16, align_bytes=64)
 
             oT_ps = psum_words.tile([P, PAIR, 2, P], F32)
@@ -114,18 +114,20 @@ def tile_gatblock_pa_t_kernel(
                 out=grouped[:, PROJ].bitcast(F32).rearrange("p r (c u) -> p r c u", u=2),
                 in_=oT_ps[:].rearrange("p r u c -> p r c u"),
             )
-
-            for s in range(PAIR):
-                aggT_ps = psum_agg.tile([P, PACK, P], F32)
-                for t in range(PACK):
-                    nc.tensor.matmul(
-                        aggT_ps[:, t, :], lhsT=h_sb[:, s, t:D:PACK], rhs=aT[:], start=True, stop=True
-                    )
-                nc.scalar.copy(
-                    out=grouped[:, GCN, :, s * D // PAIR : (s + 1) * D // PAIR].rearrange("p r (c t) -> p r c t", t=PACK),
-                    in_=aggT_ps[:].rearrange("p t (c r) -> p r c t", r=PAIR),
-                )
             grouped_tiles[k] = grouped
+
+        def mix(k, s):
+            h_sb, o_sb = loaded[k]
+            grouped = grouped_tiles[k]
+            aggT_ps = psum_agg.tile([P, PACK, P], F32)
+            for t in range(PACK):
+                nc.tensor.matmul(
+                    aggT_ps[:, t, :], lhsT=h_sb[:, s, t:D:PACK], rhs=aT[:], start=True, stop=True
+                )
+            nc.scalar.copy(
+                out=grouped[:, GCN, :, s * D // PAIR : (s + 1) * D // PAIR].rearrange("p r (c t) -> p r c t", t=PACK),
+                in_=aggT_ps[:].rearrange("p t (c r) -> p r c t", r=PAIR),
+            )
 
         def quantise(k):
             grouped = grouped_tiles.pop(k)
@@ -176,8 +178,12 @@ def tile_gatblock_pa_t_kernel(
             if i >= 3:
                 epilogue(i - 3)
             if i < N_PAIRS:
-                transpose_and_mix(i)
+                transposes(i)
+                mix(i, 0)
             if 1 <= i <= N_PAIRS:
                 quantise(i - 1)
             if 2 <= i <= N_PAIRS + 1:
                 multiply(i - 2)
+            if i < N_PAIRS:
+                mix(i, 1)
+                loaded.pop(i)

@@ -44,9 +44,9 @@ def tile_gatblock_pa_t_kernel(
         const = stack.enter_context(tc.tile_pool(name="const", bufs=1))
         loads = stack.enter_context(tc.tile_pool(name="loads", bufs=AHEAD + 2))
         work = stack.enter_context(tc.tile_pool(name="work", bufs=4))
-        psum_agg = stack.enter_context(tc.psum_pool(name="psum_agg", bufs=4))
+        psum_agg = stack.enter_context(tc.psum_pool(name="psum_agg", bufs=2))
         psum_words = stack.enter_context(tc.psum_pool(name="psum_words", bufs=2))
-        psum_out = stack.enter_context(tc.psum_pool(name="psum_out", bufs=1))
+        psum_out = stack.enter_context(tc.psum_pool(name="psum_out", bufs=2))
         stack.enter_context(tc.manual_schedule())
 
         loaded = {}

@@ -58,14 +58,20 @@ def tile_gatblock_pa_t_kernel(
         out_rows = out.flatten_outer_dims().rearrange("(k p r) n -> k p r n", p=P, r=PAIR)
 
         def load(k):
-            h_sb = loads.tile([P, PAIR, D], BF16)
-            nc.sync.dma_start(out=h_sb[:], in_=h_norm[k * PAIR : (k + 1) * PAIR].rearrange("b j d -> j b d"))
             o_sb = loads.tile([P, PAIR, D], BF16)
             nc.sync.dma_start(out=o_sb[:], in_=o_rows[k])
+            h_sb = loads.tile([P, PAIR, D], BF16)
+            nc.sync.dma_start(out=h_sb[:], in_=h_norm[k * PAIR : (k + 1) * PAIR].rearrange("b j d -> j b d"))
             loaded[k] = (h_sb, o_sb)
 
         a_sb = const.tile([P, P], BF16)
         nc.sync.dma_start(out=a_sb[:], in_=a_gcn)
+        rows_bf = const.tile([P, 2, DO], BF16)
+        nc.vector.memset(rows_bf[:], 0.0)
+        nc.scalar.dma_start(out=rows_bf[0:1, 0, :], in_=b_proj.rearrange("(o n) -> o n", o=1))
+        nc.scalar.dma_start(out=rows_bf[0:1, 1, :], in_=gcn_m.rearrange("(o n) -> o n", o=1))
+        ones_bf = const.tile([P, P], BF16)
+        nc.vector.memset(ones_bf[:], 1.0)
         load(0)
         load(1)
 
@@ -92,14 +98,20 @@ def tile_gatblock_pa_t_kernel(
         aT = const.tile([P, P], BF16)
         nc.vector.tensor_copy(out=aT[:], in_=aT_ps[:])
 
-        bias_bf = const.tile([P, DO], BF16)
-        nc.scalar.dma_start(out=bias_bf[:], in_=b_proj.partition_broadcast(P))
-        gain_bf = const.tile([P, DO], BF16)
-        nc.scalar.dma_start(out=gain_bf[:], in_=gcn_m.partition_broadcast(P))
-        bias = const.tile([P, DO], F32)
-        nc.vector.tensor_copy(out=bias[:], in_=bias_bf[:])
-        gain = const.tile([P, DO], F32)
-        nc.vector.tensor_copy(out=gain[:], in_=gain_bf[:])
+        repeated = const.tile([P, 2, DO], F32)
+        bias = repeated[:, 0, :]
+        gain = repeated[:, 1, :]
+
+        def repeat_rows():
+            repeated_ps = psum_out.tile([P, 2, DO], F32, tag="g_ps")
+            nc.tensor.matmul(
+                repeated_ps[:].rearrange("p v n -> p (v n)"),
+                lhsT=ones_bf[:],
+                rhs=rows_bf[:].rearrange("p v n -> p (v n)"),
+                start=True,
+                stop=True,
+            )
+            nc.vector.tensor_copy(out=repeated[:], in_=repeated_ps[:])
 
         def transposes(k):
             h_sb, o_sb = loaded[k]
@@ -162,11 +174,11 @@ def tile_gatblock_pa_t_kernel(
             g_ps, o_ps = products.pop(k)
             g_scaled = work.tile([P, PAIR, DO], F32)
             nc.vector.tensor_tensor(
-                out=g_scaled[:], in0=g_ps[:], in1=gain[:].unsqueeze(1).to_broadcast([P, PAIR, DO]), op=MULT
+                out=g_scaled[:], in0=g_ps[:], in1=gain.unsqueeze(1).to_broadcast([P, PAIR, DO]), op=MULT
             )
             o_biased = work.tile([P, PAIR, DO], F32)
             nc.vector.tensor_tensor(
-                out=o_biased[:], in0=o_ps[:], in1=bias[:].unsqueeze(1).to_broadcast([P, PAIR, DO]), op=ADD
+                out=o_biased[:], in0=o_ps[:], in1=bias.unsqueeze(1).to_broadcast([P, PAIR, DO]), op=ADD
             )
             result = work.tile([P, PAIR, DO], F32)
             nc.gpsimd.tensor_tensor(out=result[:], in0=g_scaled[:], in1=o_biased[:], op=ADD)
@@ -177,6 +189,8 @@ def tile_gatblock_pa_t_kernel(
                 load(i + AHEAD)
             if i >= 3:
                 epilogue(i - 3)
+            if i == 2:
+                repeat_rows()
             if i < N_PAIRS:
                 transposes(i)
                 mix(i, 0)

@@ -177,12 +177,19 @@ def tile_gatblock_pa_t_kernel(
                 out=g_scaled[:], in0=g_ps[:], in1=gain.unsqueeze(1).to_broadcast([P, PAIR, DO]), op=MULT
             )
             o_biased = work.tile([P, PAIR, DO], F32)
-            nc.vector.tensor_tensor(
-                out=o_biased[:], in0=o_ps[:], in1=bias.unsqueeze(1).to_broadcast([P, PAIR, DO]), op=ADD
-            )
             result = work.tile([P, PAIR, DO], F32)
-            nc.gpsimd.tensor_tensor(out=result[:], in0=g_scaled[:], in1=o_biased[:], op=ADD)
-            nc.sync.dma_start(out=out_rows[k], in_=result[:])
+            if k < N_PAIRS - 1:
+                nc.vector.tensor_tensor(
+                    out=o_biased[:], in0=o_ps[:], in1=bias.unsqueeze(1).to_broadcast([P, PAIR, DO]), op=ADD
+                )
+                nc.gpsimd.tensor_tensor(out=result[:], in0=g_scaled[:], in1=o_biased[:], op=ADD)
+                nc.sync.dma_start(out=out_rows[k], in_=result[:])
+            else:
+                for r in range(PAIR):
+                    nc.vector.tensor_tensor(out=o_biased[:, r, :], in0=o_ps[:, r, :], in1=bias, op=ADD)
+                for r in range(PAIR):
+                    nc.vector.tensor_tensor(out=result[:, r, :], in0=g_scaled[:, r, :], in1=o_biased[:, r, :], op=ADD)
+                    nc.sync.dma_start(out=out_rows[k][:, r, :], in_=result[:, r, :])
 
         for i in range(N_PAIRS + 3):
             if i + AHEAD < N_PAIRS:

@@ -21,6 +21,7 @@ DO = 256
 PAIR = 2
 N_PAIRS = SAMPLES // PAIR
 AHEAD = 6
+FIRST = 3
 PROJ, GCN = 0, 1
 
 FLOPS = 2 * SAMPLES * P * D * DO * 2 + 2 * SAMPLES * P * P * D
@@ -68,24 +69,24 @@ def tile_gatblock_pa_t_kernel(
         nc.sync.dma_start(out=a_sb[:], in_=a_gcn)
         rows_bf = const.tile([P, 2, DO], BF16)
         nc.vector.memset(rows_bf[:], 0.0)
-        nc.scalar.dma_start(out=rows_bf[0:1, 0, :], in_=b_proj.rearrange("(o n) -> o n", o=1))
-        nc.scalar.dma_start(out=rows_bf[0:1, 1, :], in_=gcn_m.rearrange("(o n) -> o n", o=1))
         ones_bf = const.tile([P, P], BF16)
         nc.vector.memset(ones_bf[:], 1.0)
-        load(0)
-        load(1)
+        for k in range(FIRST):
+            load(k)
 
         w_words = const.tile([P, 2, 2 * DO], U8, align_bytes=64)
         w_planes = const.tile([P, 2, DO], U8, align_bytes=64)
         nc.vector.memset(w_planes[:].rearrange("p w n -> p (w n)").bitcast(I32), 0)
-        for branch, words, scales in ((PROJ, w_proj_words, w_proj_scales), (GCN, gcn_w_words, gcn_w_scales)):
+        for branch, words, scales in ((GCN, gcn_w_words, gcn_w_scales), (PROJ, w_proj_words, w_proj_scales)):
             nc.sync.dma_start(out=w_words[:, branch, :].bitcast(I32), in_=words[0].bitcast(I32))
             for quadrant in range(4):
                 nc.sync.dma_start(
                     out=w_planes[32 * quadrant : 32 * quadrant + 4, branch, :].bitcast(I32),
                     in_=scales[0, 4 * quadrant : 4 * quadrant + 4, :].bitcast(I32),
                 )
-        for k in range(2, AHEAD):
+        nc.sync.dma_start(out=rows_bf[0:1, 0, :], in_=b_proj.rearrange("(o n) -> o n", o=1))
+        nc.sync.dma_start(out=rows_bf[0:1, 1, :], in_=gcn_m.rearrange("(o n) -> o n", o=1))
+        for k in range(FIRST, AHEAD):
             load(k)
 
         ident_bf = const.tile([P, P], BF16)
@@ -103,7 +104,7 @@ def tile_gatblock_pa_t_kernel(
         gain = repeated[:, 1, :]
 
         def repeat_rows():
-            repeated_ps = psum_out.tile([P, 2, DO], F32, tag="g_ps")
+            repeated_ps = psum_words.tile([P, 2, DO], F32, tag="oT_ps")
             nc.tensor.matmul(
                 repeated_ps[:].rearrange("p v n -> p (v n)"),
                 lhsT=ones_bf[:],
@@ -194,10 +195,10 @@ def tile_gatblock_pa_t_kernel(
         for i in range(N_PAIRS + 3):
             if i + AHEAD < N_PAIRS:
                 load(i + AHEAD)
+            if i == 3:
+                repeat_rows()
             if i >= 3:
                 epilogue(i - 3)
-            if i == 2:
-                repeat_rows()
             if i < N_PAIRS:
                 transposes(i)
                 mix(i, 0)

@@ -52,6 +52,7 @@ def tile_gatblock_pa_t_kernel(
 
         loaded = {}
         grouped_tiles = {}
+        agg_tiles = {}
         quantised = {}
         products = {}
 
@@ -132,15 +133,18 @@ def tile_gatblock_pa_t_kernel(
         def mix(k, s):
             h_sb, o_sb = loaded[k]
             grouped = grouped_tiles[k]
-            aggT_ps = psum_agg.tile([P, PACK, P], F32)
+            if s == 0:
+                agg_tiles[k] = psum_agg.tile([P, PACK, PAIR * P], BF16, name="aggT_ps")
+            aggT_ps = agg_tiles[k]
             for t in range(PACK):
                 nc.tensor.matmul(
-                    aggT_ps[:, t, :], lhsT=h_sb[:, s, t:D:PACK], rhs=aT[:], start=True, stop=True
+                    aggT_ps[:, t, s * P : (s + 1) * P], lhsT=h_sb[:, s, t:D:PACK], rhs=aT[:], start=True, stop=True
                 )
-            nc.scalar.copy(
-                out=grouped[:, GCN, :, s * D // PAIR : (s + 1) * D // PAIR].rearrange("p r (c t) -> p r c t", t=PACK),
-                in_=aggT_ps[:].rearrange("p t (c r) -> p r c t", r=PAIR),
-            )
+            if s == PAIR - 1:
+                nc.scalar.copy(
+                    out=grouped[:, GCN].rearrange("p r (c t) -> p r c t", t=PACK),
+                    in_=agg_tiles.pop(k)[:].rearrange("p t (c r) -> p r c t", r=PAIR),
+                )
 
         def quantise(k):
             grouped = grouped_tiles.pop(k)

@@ -20,7 +20,7 @@ D = 512
 DO = 256
 PAIR = 2
 N_PAIRS = SAMPLES // PAIR
-AHEAD = 6
+AHEAD = 4
 FIRST = 3
 PROJ, GCN = 0, 1
 
@@ -44,7 +44,7 @@ def tile_gatblock_pa_t_kernel(
     with ExitStack() as stack:
         const = stack.enter_context(tc.tile_pool(name="const", bufs=1))
         loads = stack.enter_context(tc.tile_pool(name="loads", bufs=AHEAD + 2))
-        work = stack.enter_context(tc.tile_pool(name="work", bufs=4))
+        work = stack.enter_context(tc.tile_pool(name="work", bufs=8))
         psum_agg = stack.enter_context(tc.psum_pool(name="psum_agg", bufs=2))
         psum_words = stack.enter_context(tc.psum_pool(name="psum_words", bufs=2))
         psum_out = stack.enter_context(tc.psum_pool(name="psum_out", bufs=2))

from contextlib import ExitStack

import concourse.mybir as mybir
from concourse.masks import make_identity

BF16 = mybir.dt.bfloat16
F32 = mybir.dt.float32
I32 = mybir.dt.int32
U8 = mybir.dt.uint8
U32 = mybir.dt.uint32
FP8X4 = mybir.dt.float8_e4m3fn_x4
FP4X4 = mybir.dt.float4_e2m1fn_x4
MULT = mybir.AluOpType.mult
ADD = mybir.AluOpType.add

P = 128
PACK = 4
SAMPLES = 64
D = 512
DO = 256
PAIR = 2
N_PAIRS = SAMPLES // PAIR
AHEAD = 4
FIRST = 3
PROJ, GCN = 0, 1

FLOPS = 2 * SAMPLES * P * D * DO * 2 + 2 * SAMPLES * P * P * D


def tile_gatblock_pa_t_kernel(
    tc,
    h_norm,
    o_attn,
    a_gcn,
    w_proj_words,
    w_proj_scales,
    b_proj,
    gcn_w_words,
    gcn_w_scales,
    gcn_m,
    out,
):
    nc = tc.nc
    with ExitStack() as stack:
        const = stack.enter_context(tc.tile_pool(name="const", bufs=1))
        loads = stack.enter_context(tc.tile_pool(name="loads", bufs=AHEAD + 2))
        work = stack.enter_context(tc.tile_pool(name="work", bufs=8))
        psum_agg = stack.enter_context(tc.psum_pool(name="psum_agg", bufs=2))
        psum_words = stack.enter_context(tc.psum_pool(name="psum_words", bufs=2))
        psum_out = stack.enter_context(tc.psum_pool(name="psum_out", bufs=2))
        stack.enter_context(tc.manual_schedule())

        loaded = {}
        grouped_tiles = {}
        agg_tiles = {}
        quantised = {}
        products = {}

        o_rows = o_attn.flatten_outer_dims().rearrange("(k p r) d -> k p r d", p=P, r=PAIR)
        out_rows = out.flatten_outer_dims().rearrange("(k p r) n -> k p r n", p=P, r=PAIR)

        def load(k):
            o_sb = loads.tile([P, PAIR, D], BF16)
            nc.sync.dma_start(out=o_sb[:], in_=o_rows[k])
            h_sb = loads.tile([P, PAIR, D], BF16)
            nc.sync.dma_start(out=h_sb[:], in_=h_norm[k * PAIR : (k + 1) * PAIR].rearrange("b j d -> j b d"))
            loaded[k] = (h_sb, o_sb)

        a_sb = const.tile([P, P], BF16)
        nc.sync.dma_start(out=a_sb[:], in_=a_gcn)
        rows_bf = const.tile([P, 2, DO], BF16)
        nc.vector.memset(rows_bf[:], 0.0)
        ones_bf = const.tile([P, P], BF16)
        nc.vector.memset(ones_bf[:], 1.0)
        for k in range(FIRST):
            load(k)

        w_words = const.tile([P, 2, 2 * DO], U8, align_bytes=64)
        w_planes = const.tile([P, 2, DO], U8, align_bytes=64)
        nc.vector.memset(w_planes[:].rearrange("p w n -> p (w n)").bitcast(I32), 0)
        for branch, words, scales in ((GCN, gcn_w_words, gcn_w_scales), (PROJ, w_proj_words, w_proj_scales)):
            nc.sync.dma_start(out=w_words[:, branch, :].bitcast(I32), in_=words[0].bitcast(I32))
            for quadrant in range(4):
                nc.sync.dma_start(
                    out=w_planes[32 * quadrant : 32 * quadrant + 4, branch, :].bitcast(I32),
                    in_=scales[0, 4 * quadrant : 4 * quadrant + 4, :].bitcast(I32),
                )
        nc.sync.dma_start(out=rows_bf[0:1, 0, :], in_=b_proj.rearrange("(o n) -> o n", o=1))
        nc.sync.dma_start(out=rows_bf[0:1, 1, :], in_=gcn_m.rearrange("(o n) -> o n", o=1))
        for k in range(FIRST, AHEAD):
            load(k)

        ident_bf = const.tile([P, P], BF16)
        make_identity(nc, ident_bf[:])
        ident_f32 = const.tile([P, P], F32)
        make_identity(nc, ident_f32[:])

        aT_ps = psum_words.tile([P, P], BF16, tag="oT_ps")
        nc.tensor.transpose(aT_ps[:], a_sb[:], ident_bf[:])
        aT = const.tile([P, P], BF16)
        nc.vector.tensor_copy(out=aT[:], in_=aT_ps[:])

        repeated = const.tile([P, 2, DO], F32)
        bias = repeated[:, 0, :]
        gain = repeated[:, 1, :]

        def repeat_rows():
            repeated_ps = psum_words.tile([P, 2, DO], F32, tag="oT_ps")
            nc.tensor.matmul(
                repeated_ps[:].rearrange("p v n -> p (v n)"),
                lhsT=ones_bf[:],
                rhs=rows_bf[:].rearrange("p v n -> p (v n)"),
                start=True,
                stop=True,
            )
            nc.vector.tensor_copy(out=repeated[:], in_=repeated_ps[:])

        def transposes(k):
            h_sb, o_sb = loaded[k]
            grouped = work.tile([P, 2, PAIR, D], BF16, align_bytes=64)

            oT_ps = psum_words.tile([P, PAIR, 2, P], F32)
            for r in range(PAIR):
                o_words = o_sb[:, r, :].bitcast(F32)
                for u in range(2):
                    nc.tensor.transpose(oT_ps[:, r, u, :], o_words[:, u : D // 2 : 2], ident_f32[:])
            nc.scalar.copy(
                out=grouped[:, PROJ].bitcast(F32).rearrange("p r (c u) -> p r c u", u=2),
                in_=oT_ps[:].rearrange("p r u c -> p r c u"),
            )
            grouped_tiles[k] = grouped

        def mix(k, s):
            h_sb, o_sb = loaded[k]
            grouped = grouped_tiles[k]
            if s == 0:
                agg_tiles[k] = psum_agg.tile([P, PACK, PAIR * P], BF16, name="aggT_ps")
            aggT_ps = agg_tiles[k]
            for t in range(PACK):
                nc.tensor.matmul(
                    aggT_ps[:, t, s * P : (s + 1) * P], lhsT=h_sb[:, s, t:D:PACK], rhs=aT[:], start=True, stop=True
                )
            if s == PAIR - 1:
                nc.scalar.copy(
                    out=grouped[:, GCN].rearrange("p r (c t) -> p r c t", t=PACK),
                    in_=agg_tiles.pop(k)[:].rearrange("p t (c r) -> p r c t", r=PAIR),
                )

        def quantise(k):
            grouped = grouped_tiles.pop(k)
            codes = work.tile([P, 2 * PAIR * P], U32, align_bytes=64)
            scales = work.tile([P, 2 * PAIR * P], U8, align_bytes=64)
            nc.vector.quantize_mx(
                out=codes[:].bitcast(FP8X4),
                scales=scales[:],
                in_=grouped[:].rearrange("p a r k -> p (a r k)"),
            )
            quantised[k] = (codes, scales)

        def multiply(k):
            codes, scales = quantised.pop(k)
            g_ps = psum_out.tile([P, PAIR, DO], F32)
            o_ps = psum_out.tile([P, PAIR, DO], F32)
            for branch, product in ((GCN, g_ps), (PROJ, o_ps)):
                for r in range(PAIR):
                    half = slice((branch * PAIR + r) * P, (branch * PAIR + r + 1) * P)
                    nc.tensor.matmul_mx(
                        out=product[:, r, :],
                        lhsT=codes[:, half].bitcast(FP8X4),
                        lhsT_scale=scales[:, half],
                        rhs=w_words[:, branch, :].bitcast(FP4X4),
                        rhs_scale=w_planes[:, branch, :],
                        start=True,
                        stop=True,
                    )
            products[k] = (g_ps, o_ps)

        def epilogue(k):
            g_ps, o_ps = products.pop(k)
            g_scaled = work.tile([P, PAIR, DO], F32)
            nc.vector.tensor_tensor(
                out=g_scaled[:], in0=g_ps[:], in1=gain.unsqueeze(1).to_broadcast([P, PAIR, DO]), op=MULT
            )
            o_biased = work.tile([P, PAIR, DO], F32)
            result = work.tile([P, PAIR, DO], F32)
            if k < N_PAIRS - 1:
                nc.vector.tensor_tensor(
                    out=o_biased[:], in0=o_ps[:], in1=bias.unsqueeze(1).to_broadcast([P, PAIR, DO]), op=ADD
                )
                nc.gpsimd.tensor_tensor(out=result[:], in0=g_scaled[:], in1=o_biased[:], op=ADD)
                nc.sync.dma_start(out=out_rows[k], in_=result[:])
            else:
                for r in range(PAIR):
                    nc.vector.tensor_tensor(out=o_biased[:, r, :], in0=o_ps[:, r, :], in1=bias, op=ADD)
                for r in range(PAIR):
                    nc.vector.tensor_tensor(out=result[:, r, :], in0=g_scaled[:, r, :], in1=o_biased[:, r, :], op=ADD)
                    nc.sync.dma_start(out=out_rows[k][:, r, :], in_=result[:, r, :])

        for i in range(N_PAIRS + 3):
            if i + AHEAD < N_PAIRS:
                load(i + AHEAD)
            if i == 3:
                repeat_rows()
            if i >= 3:
                epilogue(i - 3)
            if i < N_PAIRS:
                transposes(i)
                mix(i, 0)
            if 1 <= i <= N_PAIRS:
                quantise(i - 1)
            if 2 <= i <= N_PAIRS + 1:
                multiply(i - 2)
            if i < N_PAIRS:
                mix(i, 1)
                loaded.pop(i)
